import numpy as np
import ml_dtypes


def mxq(x, axis, fmt="e4m3"):
    dtype, down = {"e4m3": (ml_dtypes.float8_e4m3fn, 7), "e5m2": (ml_dtypes.float8_e5m2, 14)}[fmt]
    v = np.moveaxis(np.asarray(x, np.float32).astype(ml_dtypes.bfloat16).astype(np.float64), axis, -1)
    blocks = v.reshape(v.shape[:-1] + (-1, 32))
    amax = np.abs(blocks).max(-1, keepdims=True)
    byte = np.maximum(np.where(amax > 0, np.frexp(amax)[1] - 1 + 127, 0) - down, 1)
    scale = np.exp2(byte - 127.0)
    codes = (blocks / scale).astype(np.float32).astype(dtype).astype(np.float64)
    return np.moveaxis((codes * scale).reshape(v.shape), -1, axis)


WIDE = False


def mx_kscale(k):
    if not WIDE:
        return np.ones(k)
    levels = np.array([10, -10, 5, -5, 0])
    a = np.random.permutation(np.resize(levels, k // 512 * 4)).reshape(k // 512, 4)
    idx = np.arange(k)
    return np.exp2(a[idx // 512, idx % 128 // 32])


BF16 = ml_dtypes.bfloat16


def bf(x):
    return np.asarray(x, np.float32).astype(BF16)


def f64(x):
    return np.asarray(x).astype(np.float64)


B, C, D, DV, H, W = 1, 1024, 128, 512, 64, 32
N = H * W
HP, WP = H // 2, W // 2
M = HP * WP


def maxpool2(t):
    return t.reshape(B, t.shape[1], HP, 2, WP, 2).max(axis=(3, 5))


def setup_inputs():
    s = mx_kscale(C)
    return {"x": bf(np.random.standard_normal((B, C, H, W)) * s[None, :, None, None]),
            "Wq": bf(np.random.standard_normal((D, C)) * 0.5 / np.sqrt(C) / s[None, :]),
            "Wk": bf(np.random.standard_normal((D, C)) * 0.5 / np.sqrt(C) / s[None, :]),
            "Wv": bf(np.random.standard_normal((DV, C)) / np.sqrt(C) / s[None, :])}


def reference(x, Wq, Wk, Wv):
    xq = mxq(f64(x).reshape(B, C, N), 1, "e4m3")
    q = (mxq(f64(Wq), 1, "e4m3") @ xq).transpose(0, 2, 1)
    k = maxpool2((mxq(f64(Wk), 1, "e4m3") @ xq).reshape(B, D, H, W)).reshape(B, D, M)
    v = maxpool2((mxq(f64(Wv), 1, "e4m3") @ xq).reshape(B, DV, H, W)).reshape(B, DV, M)
    return q, k, v

@@ -1,0 +1,171 @@
+from contextlib import ExitStack
+
+import concourse.mybir as mybir
+from concourse.masks import make_identity
+
+BF16 = mybir.dt.bfloat16
+F32 = mybir.dt.float32
+U32 = mybir.dt.uint32
+U8 = mybir.dt.uint8
+FP8X4 = mybir.dt.float8_e4m3fn_x4
+
+P = 128
+PACK = 4
+K_PASS = P * PACK
+CHANNELS = 1024
+PASSES = CHANNELS // K_PASS
+MAP_H = 64
+MAP_W = 32
+POSITIONS = MAP_H * MAP_W
+CHUNK = 512
+CHUNKS = POSITIONS // CHUNK
+WINDOW_ROWS = CHUNK // MAP_W // 2
+POOLED = CHUNK // 4
+Q_TILES = CHUNK // P
+POOLED_TILES = 5
+WQ = POOLED_TILES
+W_TILES = POOLED_TILES + 1
+WORDS_PER_PASS = K_PASS // 2
+RUN = 4
+VECTOR_COLS = 192
+
+FLOPS = 2 * (W_TILES * P) * CHANNELS * POSITIONS
+
+
+def tile_selfattention_pa_kernel(tc, x, Wq, Wk, Wv, out_0, out_1, out_2):
+    nc = tc.nc
+
+    x_rows = x.rearrange("b (c p t) h w -> (b c) p t (h w)", p=P, t=PACK)
+    q_out = out_0[0].rearrange("(g i p) d -> g p i d", i=Q_TILES, p=P)
+    k_out = out_1[0]
+    v_out = out_2[0].rearrange("(r p) m -> p r m", p=P)
+
+    with ExitStack() as ctx:
+        keep = ctx.enter_context(tc.tile_pool(name="keep", bufs=1))
+        stage = ctx.enter_context(tc.tile_pool(name="stage", bufs=4))
+        results = ctx.enter_context(tc.tile_pool(name="results", bufs=CHUNKS))
+        psum = ctx.enter_context(tc.psum_pool(name="psum", bufs=1))
+
+        x_raw = keep.tile([P, CHUNKS, PASSES, PACK, CHUNK], BF16)
+        w_raw = keep.tile([P, W_TILES, CHANNELS], BF16)
+        x_codes = keep.tile([P, CHUNKS, PASSES, CHUNK], U32, align_bytes=64)
+        x_scales = keep.tile([P, CHUNKS, PASSES, CHUNK], U8, align_bytes=64)
+        w_codes = keep.tile([P, W_TILES, PASSES, P], U32, align_bytes=64)
+        w_scales = keep.tile([P, W_TILES, PASSES, P], U8, align_bytes=64)
+        identity = keep.tile([P, P], F32)
+
+        def load_chunk(g):
+            for c in range(PASSES):
+                nc.sync.dma_start(out=x_raw[:, g, c, :, :], in_=x_rows[c][:, :, g * CHUNK : (g + 1) * CHUNK])
+
+        load_chunk(0)
+        nc.sync.dma_start(out=w_raw[:, 0, :], in_=Wk)
+        for r in range(1, POOLED_TILES):
+            nc.sync.dma_start(out=w_raw[:, r, :], in_=Wv[(r - 1) * P : r * P, :])
+        nc.sync.dma_start(out=w_raw[:, WQ, :], in_=Wq)
+        for g in range(1, CHUNKS):
+            load_chunk(g)
+
+        make_identity(nc, identity[:])
+
+        x_grouped = {}
+
+        def regroup(g):
+            for c in range(PASSES):
+                grouped = stage.tile([P, CHUNK, PACK], BF16, align_bytes=64, name="x_grouped")
+                x_grouped[(g, c)] = grouped
+                vector_cols = slice(0, VECTOR_COLS)
+                scalar_cols = slice(VECTOR_COLS, CHUNK)
+                nc.vector.tensor_copy(
+                    out=grouped[:, vector_cols, :].rearrange("p (s i) t -> p s t i", i=RUN),
+                    in_=x_raw[:, g, c, :, vector_cols].rearrange("p t (s i) -> p s t i", i=RUN),
+                )
+                nc.scalar.copy(
+                    out=grouped[:, scalar_cols, :].rearrange("p (s i) t -> p s t i", i=RUN),
+                    in_=x_raw[:, g, c, :, scalar_cols].rearrange("p t (s i) -> p s t i", i=RUN),
+                )
+
+        def quantise(g):
+            for c in range(PASSES):
+                nc.vector.quantize_mx(
+                    out=x_codes[:, g, c, :].bitcast(FP8X4),
+                    scales=x_scales[:, g, c, :],
+                    in_=x_grouped[(g, c)][:].rearrange("p n t -> p (n t)"),
+                )
+
+        def keys_and_values(g):
+            pooled = results.tile([P, POOLED_TILES, POOLED], F32)
+            for r in range(POOLED_TILES):
+                product = psum.tile([P, CHUNK], F32, tag="wide", bufs=6)
+                for c in range(PASSES):
+                    nc.tensor.matmul_mx(
+                        out=product[:],
+                        lhsT=w_codes[:, r, c, :].bitcast(FP8X4),
+                        lhsT_scale=w_scales[:, r, c, :],
+                        rhs=x_codes[:, g, c, :].bitcast(FP8X4),
+                        rhs_scale=x_scales[:, g, c, :],
+                        start=(c == 0),
+                        stop=(c == PASSES - 1),
+                    )
+                nc.vector.tensor_reduce(
+                    out=pooled[:, r, :].rearrange("p (hp wp) -> p hp wp", hp=WINDOW_ROWS),
+                    in_=product[:].rearrange("p (hp a wp b) -> p hp wp a b", hp=WINDOW_ROWS, a=2, b=2),
+                    axis=mybir.AxisListType.XY,
+                    op=mybir.AluOpType.max,
+                )
+            m_cols = slice(g * POOLED, (g + 1) * POOLED)
+            nc.sync.dma_start(out=k_out[:, m_cols], in_=pooled[:, 0, :])
+            nc.sync.dma_start(out=v_out[:, :, m_cols], in_=pooled[:, 1:POOLED_TILES, :])
+
+        def queries(g):
+            q_sums = psum.tile([P, Q_TILES, P], F32, tag="narrow", bufs=2)
+            for i in range(Q_TILES):
+                n_cols = slice(i * P, (i + 1) * P)
+                for c in range(PASSES):
+                    nc.tensor.matmul_mx(
+                        out=q_sums[:, i, :],
+                        lhsT=x_codes[:, g, c, n_cols].bitcast(FP8X4),
+                        lhsT_scale=x_scales[:, g, c, n_cols],
+                        rhs=w_codes[:, WQ, c, :].bitcast(FP8X4),
+                        rhs_scale=w_scales[:, WQ, c, :],
+                        start=(c == 0),
+                        stop=(c == PASSES - 1),
+                    )
+            q_rows = results.tile([P, Q_TILES, P], F32)
+            nc.scalar.copy(out=q_rows[:], in_=q_sums[:])
+            nc.sync.dma_start(out=q_out[g], in_=q_rows[:])
+
+        regroup(0)
+
+        flipped = []
+        for r in range(W_TILES):
+            w_words = w_raw[:, r, :].bitcast(F32)
+            bank = psum.tile([P, PASSES, 2, P], F32, tag="wide", bufs=6, name="flipped")
+            flipped.append(bank)
+            for c in range(PASSES):
+                for u in range(2):
+                    nc.tensor.transpose(
+                        bank[:, c, u, :],
+                        w_words[:, c * WORDS_PER_PASS + u : (c + 1) * WORDS_PER_PASS : 2],
+                        identity[:],
+                    )
+        quantise(0)
+        for r in range(W_TILES):
+            w_grouped = stage.tile([P, PASSES * P * PACK], BF16, align_bytes=64)
+            nc.scalar.copy(
+                out=w_grouped[:].bitcast(F32).rearrange("p (c d u) -> p c d u", c=PASSES, u=2),
+                in_=flipped[r][:].rearrange("p c u d -> p c d u"),
+            )
+            nc.vector.quantize_mx(
+                out=w_codes[:, r, :, :].rearrange("p c d -> p (c d)").bitcast(FP8X4),
+                scales=w_scales[:, r, :, :].rearrange("p c d -> p (c d)"),
+                in_=w_grouped[:],
+            )
+
+        for g in range(CHUNKS):
+            if g + 1 < CHUNKS:
+                regroup(g + 1)
+            keys_and_values(g)
+            if g + 1 < CHUNKS:
+                quantise(g + 1)
+            queries(g)

@@ -27,7 +27,9 @@ WQ = POOLED_TILES
 W_TILES = POOLED_TILES + 1
 WORDS_PER_PASS = K_PASS // 2
 RUN = 4
-VECTOR_COLS = 192
+VECTOR_COLS = 128
+REGROUP_AT = 2
+QUANTISE_AT = 3
 
 FLOPS = 2 * (W_TILES * P) * CHANNELS * POSITIONS
 
@@ -37,12 +39,13 @@ def tile_selfattention_pa_kernel(tc, x, Wq, Wk, Wv, out_0, out_1, out_2):
 
     x_rows = x.rearrange("b (c p t) h w -> (b c) p t (h w)", p=P, t=PACK)
     q_out = out_0[0].rearrange("(g i p) d -> g p i d", i=Q_TILES, p=P)
-    k_out = out_1[0]
-    v_out = out_2[0].rearrange("(r p) m -> p r m", p=P)
+    pooled_out = [out_1[0]] + [out_2[0][r * P : (r + 1) * P, :] for r in range(POOLED_TILES - 1)]
 
     with ExitStack() as ctx:
+        ctx.enter_context(tc.manual_schedule())
         keep = ctx.enter_context(tc.tile_pool(name="keep", bufs=1))
         stage = ctx.enter_context(tc.tile_pool(name="stage", bufs=4))
+        w_stage = ctx.enter_context(tc.tile_pool(name="w_stage", bufs=W_TILES))
         results = ctx.enter_context(tc.tile_pool(name="results", bufs=CHUNKS))
         psum = ctx.enter_context(tc.psum_pool(name="psum", bufs=1))
 
@@ -70,20 +73,19 @@ def tile_selfattention_pa_kernel(tc, x, Wq, Wk, Wv, out_0, out_1, out_2):
 
         x_grouped = {}
 
-        def regroup(g):
+        def regroup(g, split):
             for c in range(PASSES):
                 grouped = stage.tile([P, CHUNK, PACK], BF16, align_bytes=64, name="x_grouped")
                 x_grouped[(g, c)] = grouped
-                vector_cols = slice(0, VECTOR_COLS)
-                scalar_cols = slice(VECTOR_COLS, CHUNK)
                 nc.vector.tensor_copy(
-                    out=grouped[:, vector_cols, :].rearrange("p (s i) t -> p s t i", i=RUN),
-                    in_=x_raw[:, g, c, :, vector_cols].rearrange("p t (s i) -> p s t i", i=RUN),
+                    out=grouped[:, :split, :].rearrange("p (s i) t -> p s t i", i=RUN),
+                    in_=x_raw[:, g, c, :, :split].rearrange("p t (s i) -> p s t i", i=RUN),
                 )
-                nc.scalar.copy(
-                    out=grouped[:, scalar_cols, :].rearrange("p (s i) t -> p s t i", i=RUN),
-                    in_=x_raw[:, g, c, :, scalar_cols].rearrange("p t (s i) -> p s t i", i=RUN),
-                )
+                if split < CHUNK:
+                    nc.scalar.copy(
+                        out=grouped[:, split:, :].rearrange("p (s i) t -> p s t i", i=RUN),
+                        in_=x_raw[:, g, c, :, split:].rearrange("p t (s i) -> p s t i", i=RUN),
+                    )
 
         def quantise(g):
             for c in range(PASSES):
@@ -93,29 +95,25 @@ def tile_selfattention_pa_kernel(tc, x, Wq, Wk, Wv, out_0, out_1, out_2):
                     in_=x_grouped[(g, c)][:].rearrange("p n t -> p (n t)"),
                 )
 
-        def keys_and_values(g):
-            pooled = results.tile([P, POOLED_TILES, POOLED], F32)
-            for r in range(POOLED_TILES):
-                product = psum.tile([P, CHUNK], F32, tag="wide", bufs=6)
-                for c in range(PASSES):
-                    nc.tensor.matmul_mx(
-                        out=product[:],
-                        lhsT=w_codes[:, r, c, :].bitcast(FP8X4),
-                        lhsT_scale=w_scales[:, r, c, :],
-                        rhs=x_codes[:, g, c, :].bitcast(FP8X4),
-                        rhs_scale=x_scales[:, g, c, :],
-                        start=(c == 0),
-                        stop=(c == PASSES - 1),
-                    )
-                nc.vector.tensor_reduce(
-                    out=pooled[:, r, :].rearrange("p (hp wp) -> p hp wp", hp=WINDOW_ROWS),
-                    in_=product[:].rearrange("p (hp a wp b) -> p hp wp a b", hp=WINDOW_ROWS, a=2, b=2),
-                    axis=mybir.AxisListType.XY,
-                    op=mybir.AluOpType.max,
+        def pooled_product(g, r, pooled):
+            product = psum.tile([P, CHUNK], F32, tag="wide", bufs=6)
+            for c in range(PASSES):
+                nc.tensor.matmul_mx(
+                    out=product[:],
+                    lhsT=w_codes[:, r, c, :].bitcast(FP8X4),
+                    lhsT_scale=w_scales[:, r, c, :],
+                    rhs=x_codes[:, g, c, :].bitcast(FP8X4),
+                    rhs_scale=x_scales[:, g, c, :],
+                    start=(c == 0),
+                    stop=(c == PASSES - 1),
                 )
-            m_cols = slice(g * POOLED, (g + 1) * POOLED)
-            nc.sync.dma_start(out=k_out[:, m_cols], in_=pooled[:, 0, :])
-            nc.sync.dma_start(out=v_out[:, :, m_cols], in_=pooled[:, 1:POOLED_TILES, :])
+            nc.vector.tensor_reduce(
+                out=pooled[:, r, :].rearrange("p (hp wp) -> p hp wp", hp=WINDOW_ROWS),
+                in_=product[:].rearrange("p (hp a wp b) -> p hp wp a b", hp=WINDOW_ROWS, a=2, b=2),
+                axis=mybir.AxisListType.XY,
+                op=mybir.AluOpType.max,
+            )
+            nc.sync.dma_start(out=pooled_out[r][:, g * POOLED : (g + 1) * POOLED], in_=pooled[:, r, :])
 
         def queries(g):
             q_sums = psum.tile([P, Q_TILES, P], F32, tag="narrow", bufs=2)
@@ -135,7 +133,7 @@ def tile_selfattention_pa_kernel(tc, x, Wq, Wk, Wv, out_0, out_1, out_2):
             nc.scalar.copy(out=q_rows[:], in_=q_sums[:])
             nc.sync.dma_start(out=q_out[g], in_=q_rows[:])
 
-        regroup(0)
+        regroup(0, CHUNK)
 
         flipped = []
         for r in range(W_TILES):
@@ -151,7 +149,7 @@ def tile_selfattention_pa_kernel(tc, x, Wq, Wk, Wv, out_0, out_1, out_2):
                     )
         quantise(0)
         for r in range(W_TILES):
-            w_grouped = stage.tile([P, PASSES * P * PACK], BF16, align_bytes=64)
+            w_grouped = w_stage.tile([P, PASSES * P * PACK], BF16, align_bytes=64)
             nc.scalar.copy(
                 out=w_grouped[:].bitcast(F32).rearrange("p (c d u) -> p c d u", c=PASSES, u=2),
                 in_=flipped[r][:].rearrange("p c u d -> p c d u"),
@@ -163,9 +161,11 @@ def tile_selfattention_pa_kernel(tc, x, Wq, Wk, Wv, out_0, out_1, out_2):
             )
 
         for g in range(CHUNKS):
-            if g + 1 < CHUNKS:
-                regroup(g + 1)
-            keys_and_values(g)
-            if g + 1 < CHUNKS:
-                quantise(g + 1)
+            pooled = results.tile([P, POOLED_TILES, POOLED], F32)
+            for r in range(POOLED_TILES):
+                if g + 1 < CHUNKS and r == REGROUP_AT:
+                    regroup(g + 1, VECTOR_COLS)
+                if g + 1 < CHUNKS and r == QUANTISE_AT:
+                    quantise(g + 1)
+                pooled_product(g, r, pooled)
             queries(g)

@@ -27,9 +27,10 @@ WQ = POOLED_TILES
 W_TILES = POOLED_TILES + 1
 WORDS_PER_PASS = K_PASS // 2
 RUN = 4
-VECTOR_COLS = 128
+GPSIMD_COLS = 128
 REGROUP_AT = 2
 QUANTISE_AT = 3
+QUERIES_AT = 2
 
 FLOPS = 2 * (W_TILES * P) * CHANNELS * POSITIONS
 
@@ -44,7 +45,7 @@ def tile_selfattention_pa_kernel(tc, x, Wq, Wk, Wv, out_0, out_1, out_2):
     with ExitStack() as ctx:
         ctx.enter_context(tc.manual_schedule())
         keep = ctx.enter_context(tc.tile_pool(name="keep", bufs=1))
-        stage = ctx.enter_context(tc.tile_pool(name="stage", bufs=4))
+        stage = ctx.enter_context(tc.tile_pool(name="stage", bufs=CHUNKS * PASSES))
         w_stage = ctx.enter_context(tc.tile_pool(name="w_stage", bufs=W_TILES))
         results = ctx.enter_context(tc.tile_pool(name="results", bufs=CHUNKS))
         psum = ctx.enter_context(tc.psum_pool(name="psum", bufs=1))
@@ -73,19 +74,31 @@ def tile_selfattention_pa_kernel(tc, x, Wq, Wk, Wv, out_0, out_1, out_2):
 
         x_grouped = {}
 
-        def regroup(g, split):
+        def regroup_on_vector(g):
             for c in range(PASSES):
                 grouped = stage.tile([P, CHUNK, PACK], BF16, align_bytes=64, name="x_grouped")
                 x_grouped[(g, c)] = grouped
                 nc.vector.tensor_copy(
-                    out=grouped[:, :split, :].rearrange("p (s i) t -> p s t i", i=RUN),
-                    in_=x_raw[:, g, c, :, :split].rearrange("p t (s i) -> p s t i", i=RUN),
+                    out=grouped[:].rearrange("p (s i) t -> p s t i", i=RUN),
+                    in_=x_raw[:, g, c, :, :].rearrange("p t (s i) -> p s t i", i=RUN),
                 )
-                if split < CHUNK:
-                    nc.scalar.copy(
-                        out=grouped[:, split:, :].rearrange("p (s i) t -> p s t i", i=RUN),
-                        in_=x_raw[:, g, c, :, split:].rearrange("p t (s i) -> p s t i", i=RUN),
-                    )
+
+        def regroup_beside_vector(g):
+            for c in range(PASSES):
+                grouped = stage.tile([P, CHUNK, PACK], BF16, align_bytes=64, name="x_grouped")
+                x_grouped[(g, c)] = grouped
+                nc.gpsimd.tensor_scalar(
+                    out=grouped[:, :GPSIMD_COLS, :],
+                    in0=x_raw[:, g, c, :, :GPSIMD_COLS].rearrange("p t n -> p n t"),
+                    scalar1=1.0,
+                    scalar2=0.0,
+                    op0=mybir.AluOpType.mult,
+                    op1=mybir.AluOpType.add,
+                )
+                nc.scalar.copy(
+                    out=grouped[:, GPSIMD_COLS:, :].rearrange("p (s i) t -> p s t i", i=RUN),
+                    in_=x_raw[:, g, c, :, GPSIMD_COLS:].rearrange("p t (s i) -> p s t i", i=RUN),
+                )
 
         def quantise(g):
             for c in range(PASSES):
@@ -133,7 +146,7 @@ def tile_selfattention_pa_kernel(tc, x, Wq, Wk, Wv, out_0, out_1, out_2):
             nc.scalar.copy(out=q_rows[:], in_=q_sums[:])
             nc.sync.dma_start(out=q_out[g], in_=q_rows[:])
 
-        regroup(0, CHUNK)
+        regroup_on_vector(0)
 
         flipped = []
         for r in range(W_TILES):
@@ -164,8 +177,9 @@ def tile_selfattention_pa_kernel(tc, x, Wq, Wk, Wv, out_0, out_1, out_2):
             pooled = results.tile([P, POOLED_TILES, POOLED], F32)
             for r in range(POOLED_TILES):
                 if g + 1 < CHUNKS and r == REGROUP_AT:
-                    regroup(g + 1, VECTOR_COLS)
+                    regroup_beside_vector(g + 1)
+                if r == QUERIES_AT:
+                    queries(g)
                 if g + 1 < CHUNKS and r == QUANTISE_AT:
                     quantise(g + 1)
                 pooled_product(g, r, pooled)
-            queries(g)

@@ -27,10 +27,10 @@ WQ = POOLED_TILES
 W_TILES = POOLED_TILES + 1
 WORDS_PER_PASS = K_PASS // 2
 RUN = 4
-GPSIMD_COLS = 128
+GPSIMD_COLS = 192
 REGROUP_AT = 2
 QUANTISE_AT = 3
-QUERIES_AT = 2
+QUERIES_AT = 3
 
 FLOPS = 2 * (W_TILES * P) * CHANNELS * POSITIONS
 

@@ -66,8 +66,9 @@ def tile_selfattention_pa_kernel(tc, x, Wq, Wk, Wv, out_0, out_1, out_2):
         nc.sync.dma_start(out=w_raw[:, 0, :], in_=Wk)
         for r in range(1, POOLED_TILES):
             nc.sync.dma_start(out=w_raw[:, r, :], in_=Wv[(r - 1) * P : r * P, :])
+        load_chunk(1)
         nc.sync.dma_start(out=w_raw[:, WQ, :], in_=Wq)
-        for g in range(1, CHUNKS):
+        for g in range(2, CHUNKS):
             load_chunk(g)
 
         make_identity(nc, identity[:])
@@ -148,11 +149,13 @@ def tile_selfattention_pa_kernel(tc, x, Wq, Wk, Wv, out_0, out_1, out_2):
 
         regroup_on_vector(0)
 
-        flipped = []
-        for r in range(W_TILES):
+        flipped = {}
+        w_grouped = {}
+
+        def flip_weights(r):
             w_words = w_raw[:, r, :].bitcast(F32)
             bank = psum.tile([P, PASSES, 2, P], F32, tag="wide", bufs=6, name="flipped")
-            flipped.append(bank)
+            flipped[r] = bank
             for c in range(PASSES):
                 for u in range(2):
                     nc.tensor.transpose(
@@ -160,26 +163,43 @@ def tile_selfattention_pa_kernel(tc, x, Wq, Wk, Wv, out_0, out_1, out_2):
                         w_words[:, c * WORDS_PER_PASS + u : (c + 1) * WORDS_PER_PASS : 2],
                         identity[:],
                     )
-        quantise(0)
-        for r in range(W_TILES):
-            w_grouped = w_stage.tile([P, PASSES * P * PACK], BF16, align_bytes=64)
+
+        def group_weights(r):
+            grouped = w_stage.tile([P, PASSES * P * PACK], BF16, align_bytes=64, name="w_grouped")
+            w_grouped[r] = grouped
             nc.scalar.copy(
-                out=w_grouped[:].bitcast(F32).rearrange("p (c d u) -> p c d u", c=PASSES, u=2),
+                out=grouped[:].bitcast(F32).rearrange("p (c d u) -> p c d u", c=PASSES, u=2),
                 in_=flipped[r][:].rearrange("p c u d -> p c d u"),
             )
+
+        def quantise_weights(r):
             nc.vector.quantize_mx(
                 out=w_codes[:, r, :, :].rearrange("p c d -> p (c d)").bitcast(FP8X4),
                 scales=w_scales[:, r, :, :].rearrange("p c d -> p (c d)"),
-                in_=w_grouped[:],
+                in_=w_grouped[r][:],
             )
+
+        for r in range(POOLED_TILES):
+            flip_weights(r)
+        quantise(0)
+        for r in range(POOLED_TILES):
+            group_weights(r)
+            quantise_weights(r)
 
         for g in range(CHUNKS):
             pooled = results.tile([P, POOLED_TILES, POOLED], F32)
             for r in range(POOLED_TILES):
                 if g + 1 < CHUNKS and r == REGROUP_AT:
                     regroup_beside_vector(g + 1)
-                if r == QUERIES_AT:
+                if g == 1 and r == 1:
+                    quantise_weights(WQ)
+                if r == QUERIES_AT and g == 1:
+                    queries(0)
+                if r == QUERIES_AT and g >= 1:
                     queries(g)
                 if g + 1 < CHUNKS and r == QUANTISE_AT:
                     quantise(g + 1)
                 pooled_product(g, r, pooled)
+            if g == 0:
+                flip_weights(WQ)
+                group_weights(WQ)

@@ -26,7 +26,7 @@ POOLED_TILES = 5
 WQ = POOLED_TILES
 W_TILES = POOLED_TILES + 1
 WORDS_PER_PASS = K_PASS // 2
-RUN = 4
+RUN = 8
 GPSIMD_COLS = 192
 REGROUP_AT = 2
 QUANTISE_AT = 3

@@ -31,6 +31,9 @@ GPSIMD_COLS = 192
 REGROUP_AT = 2
 QUANTISE_AT = 3
 QUERIES_AT = 3
+WARM_UP = 14
+WARM_BETWEEN = 1
+WARM_BEFORE_PRODUCTS = 2
 
 FLOPS = 2 * (W_TILES * P) * CHANNELS * POSITIONS
 
@@ -57,6 +60,7 @@ def tile_selfattention_pa_kernel(tc, x, Wq, Wk, Wv, out_0, out_1, out_2):
         w_codes = keep.tile([P, W_TILES, PASSES, P], U32, align_bytes=64)
         w_scales = keep.tile([P, W_TILES, PASSES, P], U8, align_bytes=64)
         identity = keep.tile([P, P], F32)
+        zeros = keep.tile([P, P], F32)
 
         def load_chunk(g):
             for c in range(PASSES):
@@ -72,6 +76,15 @@ def tile_selfattention_pa_kernel(tc, x, Wq, Wk, Wv, out_0, out_1, out_2):
             load_chunk(g)
 
         make_identity(nc, identity[:])
+        nc.vector.memset(zeros[:], 0.0)
+
+        unread = psum.tile([P, Q_TILES, P], F32, tag="narrow", bufs=2, name="unread")
+
+        def keep_warm(count):
+            for i in range(count):
+                nc.tensor.matmul(unread[:, i % Q_TILES, :], lhsT=zeros[:], rhs=zeros[:], start=True, stop=True)
+
+        keep_warm(WARM_UP)
 
         x_grouped = {}
 
@@ -181,6 +194,7 @@ def tile_selfattention_pa_kernel(tc, x, Wq, Wk, Wv, out_0, out_1, out_2):
 
         for r in range(POOLED_TILES):
             flip_weights(r)
+            keep_warm(WARM_BETWEEN if r < POOLED_TILES - 1 else WARM_BEFORE_PRODUCTS)
         quantise(0)
         for r in range(POOLED_TILES):
             group_weights(r)

@@ -41,7 +41,7 @@ FLOPS = 2 * (W_TILES * P) * CHANNELS * POSITIONS
 def tile_selfattention_pa_kernel(tc, x, Wq, Wk, Wv, out_0, out_1, out_2):
     nc = tc.nc
 
-    x_rows = x.rearrange("b (c p t) h w -> (b c) p t (h w)", p=P, t=PACK)
+    x_rows = x.rearrange("b (c u p e) h w -> (b c) u p e (h w)", u=2, p=P, e=2)
     q_out = out_0[0].rearrange("(g i p) d -> g p i d", i=Q_TILES, p=P)
     pooled_out = [out_1[0]] + [out_2[0][r * P : (r + 1) * P, :] for r in range(POOLED_TILES - 1)]
 
@@ -64,7 +64,11 @@ def tile_selfattention_pa_kernel(tc, x, Wq, Wk, Wv, out_0, out_1, out_2):
 
         def load_chunk(g):
             for c in range(PASSES):
-                nc.sync.dma_start(out=x_raw[:, g, c, :, :], in_=x_rows[c][:, :, g * CHUNK : (g + 1) * CHUNK])
+                for u in range(2):
+                    nc.sync.dma_start(
+                        out=x_raw[:, g, c, 2 * u : 2 * u + 2, :],
+                        in_=x_rows[c, u][:, :, g * CHUNK : (g + 1) * CHUNK],
+                    )
 
         load_chunk(0)
         nc.sync.dma_start(out=w_raw[:, 0, :], in_=Wk)
@@ -173,7 +177,7 @@ def tile_selfattention_pa_kernel(tc, x, Wq, Wk, Wv, out_0, out_1, out_2):
                 for u in range(2):
                     nc.tensor.transpose(
                         bank[:, c, u, :],
-                        w_words[:, c * WORDS_PER_PASS + u : (c + 1) * WORDS_PER_PASS : 2],
+                        w_words[:, c * WORDS_PER_PASS + u * P : c * WORDS_PER_PASS + (u + 1) * P],
                         identity[:],
                     )
 

@@ -32,8 +32,6 @@ REGROUP_AT = 2
 QUANTISE_AT = 3
 QUERIES_AT = 3
 WARM_UP = 14
-WARM_BETWEEN = 1
-WARM_BEFORE_PRODUCTS = 2
 
 FLOPS = 2 * (W_TILES * P) * CHANNELS * POSITIONS
 
@@ -84,11 +82,8 @@ def tile_selfattention_pa_kernel(tc, x, Wq, Wk, Wv, out_0, out_1, out_2):
 
         unread = psum.tile([P, Q_TILES, P], F32, tag="narrow", bufs=2, name="unread")
 
-        def keep_warm(count):
-            for i in range(count):
-                nc.tensor.matmul(unread[:, i % Q_TILES, :], lhsT=zeros[:], rhs=zeros[:], start=True, stop=True)
-
-        keep_warm(WARM_UP)
+        for i in range(WARM_UP):
+            nc.tensor.matmul(unread[:, i % Q_TILES, :], lhsT=zeros[:], rhs=zeros[:], start=True, stop=True)
 
         x_grouped = {}
 
@@ -198,7 +193,6 @@ def tile_selfattention_pa_kernel(tc, x, Wq, Wk, Wv, out_0, out_1, out_2):
 
         for r in range(POOLED_TILES):
             flip_weights(r)
-            keep_warm(WARM_BETWEEN if r < POOLED_TILES - 1 else WARM_BEFORE_PRODUCTS)
         quantise(0)
         for r in range(POOLED_TILES):
             group_weights(r)

@@ -28,9 +28,10 @@ W_TILES = POOLED_TILES + 1
 WORDS_PER_PASS = K_PASS // 2
 RUN = 8
 GPSIMD_COLS = 192
-REGROUP_AT = 2
-QUANTISE_AT = 3
-QUERIES_AT = 3
+REGROUP_AT = {1: (0, 2), 2: (1, 2), 3: (1, 3)}
+QUANTISE_AT = {1: (0, 3), 2: (1, 2), 3: (2, 2)}
+WQ_BEHIND = (0, 2)
+QUERIES_AT = {0: (1, 2), 1: (2, 2), 2: (2, 3), 3: (3, 2)}
 WARM_UP = 14
 
 FLOPS = 2 * (W_TILES * P) * CHANNELS * POSITIONS
@@ -196,22 +197,26 @@ def tile_selfattention_pa_kernel(tc, x, Wq, Wk, Wv, out_0, out_1, out_2):
         quantise(0)
         for r in range(POOLED_TILES):
             group_weights(r)
-            quantise_weights(r)
+            if r < POOLED_TILES - 1:
+                quantise_weights(r)
 
         for g in range(CHUNKS):
             pooled = results.tile([P, POOLED_TILES, POOLED], F32)
             for r in range(POOLED_TILES):
-                if g + 1 < CHUNKS and r == REGROUP_AT:
-                    regroup_beside_vector(g + 1)
-                if g == 1 and r == 1:
+                if (g, r) == (1, 0):
                     quantise_weights(WQ)
-                if r == QUERIES_AT and g == 1:
-                    queries(0)
-                if r == QUERIES_AT and g >= 1:
-                    queries(g)
-                if g + 1 < CHUNKS and r == QUANTISE_AT:
-                    quantise(g + 1)
+                for h in range(1, CHUNKS):
+                    if REGROUP_AT[h] == (g, r):
+                        regroup_beside_vector(h)
+                for h in range(CHUNKS):
+                    if QUERIES_AT[h] == (g, r):
+                        queries(h)
+                for h in range(1, CHUNKS):
+                    if QUANTISE_AT[h] == (g, r):
+                        quantise(h)
                 pooled_product(g, r, pooled)
-            if g == 0:
-                flip_weights(WQ)
-                group_weights(WQ)
+                if (g, r) == (0, 0):
+                    quantise_weights(POOLED_TILES - 1)
+                if (g, r) == WQ_BEHIND:
+                    flip_weights(WQ)
+                    group_weights(WQ)

@@ -47,7 +47,7 @@ def tile_selfattention_pa_kernel(tc, x, Wq, Wk, Wv, out_0, out_1, out_2):
     with ExitStack() as ctx:
         ctx.enter_context(tc.manual_schedule())
         keep = ctx.enter_context(tc.tile_pool(name="keep", bufs=1))
-        stage = ctx.enter_context(tc.tile_pool(name="stage", bufs=CHUNKS * PASSES))
+        stage = ctx.enter_context(tc.tile_pool(name="stage", bufs=PASSES))
         w_stage = ctx.enter_context(tc.tile_pool(name="w_stage", bufs=W_TILES))
         results = ctx.enter_context(tc.tile_pool(name="results", bufs=CHUNKS))
         psum = ctx.enter_context(tc.psum_pool(name="psum", bufs=1))

@@ -33,6 +33,8 @@ QUANTISE_AT = {1: (0, 3), 2: (1, 2), 3: (2, 2)}
 WQ_BEHIND = (0, 2)
 QUERIES_AT = {0: (1, 2), 1: (2, 2), 2: (2, 3), 3: (3, 2)}
 WARM_UP = 14
+WARM_BETWEEN = 1
+WARM_BEFORE_WQ = 2
 
 FLOPS = 2 * (W_TILES * P) * CHANNELS * POSITIONS
 
@@ -83,8 +85,11 @@ def tile_selfattention_pa_kernel(tc, x, Wq, Wk, Wv, out_0, out_1, out_2):
 
         unread = psum.tile([P, Q_TILES, P], F32, tag="narrow", bufs=2, name="unread")
 
-        for i in range(WARM_UP):
-            nc.tensor.matmul(unread[:, i % Q_TILES, :], lhsT=zeros[:], rhs=zeros[:], start=True, stop=True)
+        def keep_warm(count):
+            for i in range(count):
+                nc.tensor.matmul(unread[:, i % Q_TILES, :], lhsT=zeros[:], rhs=zeros[:], start=True, stop=True)
+
+        keep_warm(WARM_UP)
 
         x_grouped = {}
 
@@ -194,6 +199,8 @@ def tile_selfattention_pa_kernel(tc, x, Wq, Wk, Wv, out_0, out_1, out_2):
 
         for r in range(POOLED_TILES):
             flip_weights(r)
+            if r < POOLED_TILES - 1:
+                keep_warm(WARM_BETWEEN)
         quantise(0)
         for r in range(POOLED_TILES):
             group_weights(r)
@@ -218,5 +225,6 @@ def tile_selfattention_pa_kernel(tc, x, Wq, Wk, Wv, out_0, out_1, out_2):
                 if (g, r) == (0, 0):
                     quantise_weights(POOLED_TILES - 1)
                 if (g, r) == WQ_BEHIND:
+                    keep_warm(WARM_BEFORE_WQ)
                     flip_weights(WQ)
                     group_weights(WQ)

@@ -27,14 +27,15 @@ WQ = POOLED_TILES
 W_TILES = POOLED_TILES + 1
 WORDS_PER_PASS = K_PASS // 2
 RUN = 8
+VECTOR_COLS = 352
 GPSIMD_COLS = 192
 REGROUP_AT = {1: (0, 2), 2: (1, 2), 3: (1, 3)}
 QUANTISE_AT = {1: (0, 3), 2: (1, 2), 3: (2, 2)}
 WQ_BEHIND = (0, 2)
 QUERIES_AT = {0: (1, 2), 1: (2, 2), 2: (2, 3), 3: (3, 2)}
-WARM_UP = 14
-WARM_BETWEEN = 1
-WARM_BEFORE_WQ = 2
+WARM_UP = [512] * 13
+WARM_BETWEEN = [384]
+WARM_BEFORE_WQ = [512] * 2
 
 FLOPS = 2 * (W_TILES * P) * CHANNELS * POSITIONS
 
@@ -61,7 +62,7 @@ def tile_selfattention_pa_kernel(tc, x, Wq, Wk, Wv, out_0, out_1, out_2):
         w_codes = keep.tile([P, W_TILES, PASSES, P], U32, align_bytes=64)
         w_scales = keep.tile([P, W_TILES, PASSES, P], U8, align_bytes=64)
         identity = keep.tile([P, P], F32)
-        zeros = keep.tile([P, P], F32)
+        zeros = keep.tile([P, CHUNK], BF16)
 
         def load_chunk(g):
             for c in range(PASSES):
@@ -83,24 +84,31 @@ def tile_selfattention_pa_kernel(tc, x, Wq, Wk, Wv, out_0, out_1, out_2):
         make_identity(nc, identity[:])
         nc.vector.memset(zeros[:], 0.0)
 
-        unread = psum.tile([P, Q_TILES, P], F32, tag="narrow", bufs=2, name="unread")
+        unread = []
+        for i in range(2):
+            bank = psum.tile([P, CHUNK], F32, tag="narrow", bufs=2, name="unread")
+            unread.append(bank)
 
-        def keep_warm(count):
-            for i in range(count):
-                nc.tensor.matmul(unread[:, i % Q_TILES, :], lhsT=zeros[:], rhs=zeros[:], start=True, stop=True)
+        def keep_warm(widths):
+            for i, width in enumerate(widths):
+                nc.tensor.matmul(unread[i % 2][:, :width], lhsT=zeros[:, :P], rhs=zeros[:, :width], start=True, stop=True)
 
         keep_warm(WARM_UP)
 
         x_grouped = {}
 
-        def regroup_on_vector(g):
+        def regroup_runs(copy, g, c, cols):
+            copy(
+                out=x_grouped[(g, c)][:, cols, :].rearrange("p (s i) t -> p s t i", i=RUN),
+                in_=x_raw[:, g, c, :, cols].rearrange("p t (s i) -> p s t i", i=RUN),
+            )
+
+        def regroup_with_vector(g):
             for c in range(PASSES):
                 grouped = stage.tile([P, CHUNK, PACK], BF16, align_bytes=64, name="x_grouped")
                 x_grouped[(g, c)] = grouped
-                nc.vector.tensor_copy(
-                    out=grouped[:].rearrange("p (s i) t -> p s t i", i=RUN),
-                    in_=x_raw[:, g, c, :, :].rearrange("p t (s i) -> p s t i", i=RUN),
-                )
+                regroup_runs(nc.vector.tensor_copy, g, c, slice(0, VECTOR_COLS))
+                regroup_runs(nc.scalar.copy, g, c, slice(VECTOR_COLS, CHUNK))
 
         def regroup_beside_vector(g):
             for c in range(PASSES):
@@ -114,10 +122,7 @@ def tile_selfattention_pa_kernel(tc, x, Wq, Wk, Wv, out_0, out_1, out_2):
                     op0=mybir.AluOpType.mult,
                     op1=mybir.AluOpType.add,
                 )
-                nc.scalar.copy(
-                    out=grouped[:, GPSIMD_COLS:, :].rearrange("p (s i) t -> p s t i", i=RUN),
-                    in_=x_raw[:, g, c, :, GPSIMD_COLS:].rearrange("p t (s i) -> p s t i", i=RUN),
-                )
+                regroup_runs(nc.scalar.copy, g, c, slice(GPSIMD_COLS, CHUNK))
 
         def quantise(g):
             for c in range(PASSES):
@@ -165,7 +170,7 @@ def tile_selfattention_pa_kernel(tc, x, Wq, Wk, Wv, out_0, out_1, out_2):
             nc.scalar.copy(out=q_rows[:], in_=q_sums[:])
             nc.sync.dma_start(out=q_out[g], in_=q_rows[:])
 
-        regroup_on_vector(0)
+        regroup_with_vector(0)
 
         flipped = {}
         w_grouped = {}

from contextlib import ExitStack

import concourse.mybir as mybir
from concourse.masks import make_identity

BF16 = mybir.dt.bfloat16
F32 = mybir.dt.float32
U32 = mybir.dt.uint32
U8 = mybir.dt.uint8
FP8X4 = mybir.dt.float8_e4m3fn_x4

P = 128
PACK = 4
K_PASS = P * PACK
CHANNELS = 1024
PASSES = CHANNELS // K_PASS
MAP_H = 64
MAP_W = 32
POSITIONS = MAP_H * MAP_W
CHUNK = 512
CHUNKS = POSITIONS // CHUNK
WINDOW_ROWS = CHUNK // MAP_W // 2
POOLED = CHUNK // 4
Q_TILES = CHUNK // P
POOLED_TILES = 5
WQ = POOLED_TILES
W_TILES = POOLED_TILES + 1
WORDS_PER_PASS = K_PASS // 2
RUN = 8
VECTOR_COLS = 352
GPSIMD_COLS = 192
REGROUP_AT = {1: (0, 2), 2: (1, 2), 3: (1, 3)}
QUANTISE_AT = {1: (0, 3), 2: (1, 2), 3: (2, 2)}
WQ_BEHIND = (0, 2)
QUERIES_AT = {0: (1, 2), 1: (2, 2), 2: (2, 3), 3: (3, 2)}
WARM_UP = [512] * 13
WARM_BETWEEN = [384]
WARM_BEFORE_WQ = [512] * 2

FLOPS = 2 * (W_TILES * P) * CHANNELS * POSITIONS


def tile_selfattention_pa_kernel(tc, x, Wq, Wk, Wv, out_0, out_1, out_2):
    nc = tc.nc

    x_rows = x.rearrange("b (c u p e) h w -> (b c) u p e (h w)", u=2, p=P, e=2)
    q_out = out_0[0].rearrange("(g i p) d -> g p i d", i=Q_TILES, p=P)
    pooled_out = [out_1[0]] + [out_2[0][r * P : (r + 1) * P, :] for r in range(POOLED_TILES - 1)]

    with ExitStack() as ctx:
        ctx.enter_context(tc.manual_schedule())
        keep = ctx.enter_context(tc.tile_pool(name="keep", bufs=1))
        stage = ctx.enter_context(tc.tile_pool(name="stage", bufs=PASSES))
        w_stage = ctx.enter_context(tc.tile_pool(name="w_stage", bufs=W_TILES))
        results = ctx.enter_context(tc.tile_pool(name="results", bufs=CHUNKS))
        psum = ctx.enter_context(tc.psum_pool(name="psum", bufs=1))

        x_raw = keep.tile([P, CHUNKS, PASSES, PACK, CHUNK], BF16)
        w_raw = keep.tile([P, W_TILES, CHANNELS], BF16)
        x_codes = keep.tile([P, CHUNKS, PASSES, CHUNK], U32, align_bytes=64)
        x_scales = keep.tile([P, CHUNKS, PASSES, CHUNK], U8, align_bytes=64)
        w_codes = keep.tile([P, W_TILES, PASSES, P], U32, align_bytes=64)
        w_scales = keep.tile([P, W_TILES, PASSES, P], U8, align_bytes=64)
        identity = keep.tile([P, P], F32)
        zeros = keep.tile([P, CHUNK], BF16)

        def load_chunk(g):
            for c in range(PASSES):
                for u in range(2):
                    nc.sync.dma_start(
                        out=x_raw[:, g, c, 2 * u : 2 * u + 2, :],
                        in_=x_rows[c, u][:, :, g * CHUNK : (g + 1) * CHUNK],
                    )

        load_chunk(0)
        nc.sync.dma_start(out=w_raw[:, 0, :], in_=Wk)
        for r in range(1, POOLED_TILES):
            nc.sync.dma_start(out=w_raw[:, r, :], in_=Wv[(r - 1) * P : r * P, :])
        load_chunk(1)
        nc.sync.dma_start(out=w_raw[:, WQ, :], in_=Wq)
        for g in range(2, CHUNKS):
            load_chunk(g)

        make_identity(nc, identity[:])
        nc.vector.memset(zeros[:], 0.0)

        unread = []
        for i in range(2):
            bank = psum.tile([P, CHUNK], F32, tag="narrow", bufs=2, name="unread")
            unread.append(bank)

        def keep_warm(widths):
            for i, width in enumerate(widths):
                nc.tensor.matmul(unread[i % 2][:, :width], lhsT=zeros[:, :P], rhs=zeros[:, :width], start=True, stop=True)

        keep_warm(WARM_UP)

        x_grouped = {}

        def regroup_runs(copy, g, c, cols):
            copy(
                out=x_grouped[(g, c)][:, cols, :].rearrange("p (s i) t -> p s t i", i=RUN),
                in_=x_raw[:, g, c, :, cols].rearrange("p t (s i) -> p s t i", i=RUN),
            )

        def regroup_with_vector(g):
            for c in range(PASSES):
                grouped = stage.tile([P, CHUNK, PACK], BF16, align_bytes=64, name="x_grouped")
                x_grouped[(g, c)] = grouped
                regroup_runs(nc.vector.tensor_copy, g, c, slice(0, VECTOR_COLS))
                regroup_runs(nc.scalar.copy, g, c, slice(VECTOR_COLS, CHUNK))

        def regroup_beside_vector(g):
            for c in range(PASSES):
                grouped = stage.tile([P, CHUNK, PACK], BF16, align_bytes=64, name="x_grouped")
                x_grouped[(g, c)] = grouped
                nc.gpsimd.tensor_scalar(
                    out=grouped[:, :GPSIMD_COLS, :],
                    in0=x_raw[:, g, c, :, :GPSIMD_COLS].rearrange("p t n -> p n t"),
                    scalar1=1.0,
                    scalar2=0.0,
                    op0=mybir.AluOpType.mult,
                    op1=mybir.AluOpType.add,
                )
                regroup_runs(nc.scalar.copy, g, c, slice(GPSIMD_COLS, CHUNK))

        def quantise(g):
            for c in range(PASSES):
                nc.vector.quantize_mx(
                    out=x_codes[:, g, c, :].bitcast(FP8X4),
                    scales=x_scales[:, g, c, :],
                    in_=x_grouped[(g, c)][:].rearrange("p n t -> p (n t)"),
                )

        def pooled_product(g, r, pooled):
            product = psum.tile([P, CHUNK], F32, tag="wide", bufs=6)
            for c in range(PASSES):
                nc.tensor.matmul_mx(
                    out=product[:],
                    lhsT=w_codes[:, r, c, :].bitcast(FP8X4),
                    lhsT_scale=w_scales[:, r, c, :],
                    rhs=x_codes[:, g, c, :].bitcast(FP8X4),
                    rhs_scale=x_scales[:, g, c, :],
                    start=(c == 0),
                    stop=(c == PASSES - 1),
                )
            nc.vector.tensor_reduce(
                out=pooled[:, r, :].rearrange("p (hp wp) -> p hp wp", hp=WINDOW_ROWS),
                in_=product[:].rearrange("p (hp a wp b) -> p hp wp a b", hp=WINDOW_ROWS, a=2, b=2),
                axis=mybir.AxisListType.XY,
                op=mybir.AluOpType.max,
            )
            nc.sync.dma_start(out=pooled_out[r][:, g * POOLED : (g + 1) * POOLED], in_=pooled[:, r, :])

        def queries(g):
            q_sums = psum.tile([P, Q_TILES, P], F32, tag="narrow", bufs=2)
            for i in range(Q_TILES):
                n_cols = slice(i * P, (i + 1) * P)
                for c in range(PASSES):
                    nc.tensor.matmul_mx(
                        out=q_sums[:, i, :],
                        lhsT=x_codes[:, g, c, n_cols].bitcast(FP8X4),
                        lhsT_scale=x_scales[:, g, c, n_cols],
                        rhs=w_codes[:, WQ, c, :].bitcast(FP8X4),
                        rhs_scale=w_scales[:, WQ, c, :],
                        start=(c == 0),
                        stop=(c == PASSES - 1),
                    )
            q_rows = results.tile([P, Q_TILES, P], F32)
            nc.scalar.copy(out=q_rows[:], in_=q_sums[:])
            nc.sync.dma_start(out=q_out[g], in_=q_rows[:])

        regroup_with_vector(0)

        flipped = {}
        w_grouped = {}

        def flip_weights(r):
            w_words = w_raw[:, r, :].bitcast(F32)
            bank = psum.tile([P, PASSES, 2, P], F32, tag="wide", bufs=6, name="flipped")
            flipped[r] = bank
            for c in range(PASSES):
                for u in range(2):
                    nc.tensor.transpose(
                        bank[:, c, u, :],
                        w_words[:, c * WORDS_PER_PASS + u * P : c * WORDS_PER_PASS + (u + 1) * P],
                        identity[:],
                    )

        def group_weights(r):
            grouped = w_stage.tile([P, PASSES * P * PACK], BF16, align_bytes=64, name="w_grouped")
            w_grouped[r] = grouped
            nc.scalar.copy(
                out=grouped[:].bitcast(F32).rearrange("p (c d u) -> p c d u", c=PASSES, u=2),
                in_=flipped[r][:].rearrange("p c u d -> p c d u"),
            )

        def quantise_weights(r):
            nc.vector.quantize_mx(
                out=w_codes[:, r, :, :].rearrange("p c d -> p (c d)").bitcast(FP8X4),
                scales=w_scales[:, r, :, :].rearrange("p c d -> p (c d)"),
                in_=w_grouped[r][:],
            )

        for r in range(POOLED_TILES):
            flip_weights(r)
            if r < POOLED_TILES - 1:
                keep_warm(WARM_BETWEEN)
        quantise(0)
        for r in range(POOLED_TILES):
            group_weights(r)
            if r < POOLED_TILES - 1:
                quantise_weights(r)

        for g in range(CHUNKS):
            pooled = results.tile([P, POOLED_TILES, POOLED], F32)
            for r in range(POOLED_TILES):
                if (g, r) == (1, 0):
                    quantise_weights(WQ)
                for h in range(1, CHUNKS):
                    if REGROUP_AT[h] == (g, r):
                        regroup_beside_vector(h)
                for h in range(CHUNKS):
                    if QUERIES_AT[h] == (g, r):
                        queries(h)
                for h in range(1, CHUNKS):
                    if QUANTISE_AT[h] == (g, r):
                        quantise(h)
                pooled_product(g, r, pooled)
                if (g, r) == (0, 0):
                    quantise_weights(POOLED_TILES - 1)
                if (g, r) == WQ_BEHIND:
                    keep_warm(WARM_BEFORE_WQ)
                    flip_weights(WQ)
                    group_weights(WQ)
